import numpy as np
import ml_dtypes


def mxq(x, axis, fmt="e4m3"):
    dtype, down = {"e4m3": (ml_dtypes.float8_e4m3fn, 7), "e5m2": (ml_dtypes.float8_e5m2, 14)}[fmt]
    v = np.moveaxis(np.asarray(x, np.float32).astype(ml_dtypes.bfloat16).astype(np.float64), axis, -1)
    blocks = v.reshape(v.shape[:-1] + (-1, 32))
    amax = np.abs(blocks).max(-1, keepdims=True)
    byte = np.maximum(np.where(amax > 0, np.frexp(amax)[1] - 1 + 127, 0) - down, 1)
    scale = np.exp2(byte - 127.0)
    codes = (blocks / scale).astype(np.float32).astype(dtype).astype(np.float64)
    return np.moveaxis((codes * scale).reshape(v.shape), -1, axis)


WIDE = False


def mx_kscale(k):
    if not WIDE:
        return np.ones(k)
    levels = np.array([10, -10, 5, -5, 0])
    if k % 512:
        return np.exp2(np.random.permutation(np.resize(levels, k // 32))).repeat(32)
    a = np.empty((k // 512, 16))
    for p in range(k // 512):
        a[p, :8] = np.random.permutation(np.resize(levels, 8))
        for g in range(8):
            far = levels[np.abs(levels - a[p, g]) >= 10]
            a[p, g + 8] = far[np.random.randint(len(far))]
    return np.exp2(a.ravel()).repeat(32)


BF16 = ml_dtypes.bfloat16


def bf(x):
    return np.asarray(x, np.float32).astype(BF16)


def f64(x):
    return np.asarray(x).astype(np.float64)


E2M1 = np.array([0.0, 0.5, 1.0, 1.5, 2.0, 3.0, 4.0, 6.0, -0.0, -0.5, -1.0, -1.5, -2.0, -3.0, -4.0, -6.0])


def pack_weight(w, fmt):
    k, n = w.shape
    w = f64(bf(w)).reshape(k // 32, 32, n)
    amax = np.abs(w).max(1)
    if fmt == "e4m3":
        byte = np.frexp(amax)[1] - 1 + 127 - 7
    else:
        mant, ex = np.frexp(amax / 6.0)
        byte = np.where(mant > 0.5, ex, ex - 1) + 127
    byte = np.clip(np.where(amax > 0, byte, 1), 1, 254)
    scaled = (w * np.exp2(127.0 - byte)[:, None, :]).reshape(k, n).astype(np.float32)
    by_word = np.ascontiguousarray(scaled.reshape(k // 512, 128, 4, n).transpose(0, 1, 3, 2))
    if fmt == "e4m3":
        words = by_word.astype(ml_dtypes.float8_e4m3fn).view(np.uint8)
    else:
        c = by_word.astype(ml_dtypes.float4_e2m1fn).view(np.uint8) & 0xF
        words = c[..., 0::2] | (c[..., 1::2] << 4)
    return np.ascontiguousarray(words), np.ascontiguousarray(byte.astype(np.uint8).reshape(k // 512, 16, n))


def unpack_weight(words, scales, fmt):
    g, p, n, _ = words.shape
    if fmt == "e4m3":
        vals = np.ascontiguousarray(words).view(ml_dtypes.float8_e4m3fn).astype(np.float64)
    else:
        nib = np.empty((g, p, n, 4), np.uint8)
        nib[..., 0::2] = words & 0xF
        nib[..., 1::2] = words >> 4
        vals = E2M1[nib]
    vals = vals * np.repeat(np.exp2(scales.astype(np.float64) - 127.0), 8, axis=1)[..., None]
    return vals.transpose(0, 1, 3, 2).reshape(g * 512, n)
def pack4(w):
    words, scales = pack_weight(w, "e2m1")
    return words.reshape(words.shape[0], 128, -1), scales


def unpack4(words, scales):
    return unpack_weight(words.reshape(words.shape[0], 128, -1, 2), scales, "e2m1")


B, T, D, H, HD, Q_STRIDE, WINDOW, QKV = 1, 1536, 1024, 16, 64, 4, 128, 3
NW = T // (Q_STRIDE * WINDOW)
SEQ = T // NW


def draw0():
    s = mx_kscale(SEQ)
    t = mx_kscale(D)
    g = np.exp(np.random.standard_normal((B, H, NW, SEQ // Q_STRIDE, SEQ)) * 1.3)
    vd = np.random.standard_normal((B, NW, SEQ, D)) * t / s[:, None]
    words, scales = pack4((np.random.standard_normal((D, D)) * 5.0 / np.sqrt(D) / t[None, :]).T)
    return {"attn": bf(g / g.sum(-1, keepdims=True) * s),
            "v": bf(np.ascontiguousarray(vd.reshape(B, NW, SEQ, H, HD).transpose(0, 3, 1, 2, 4))),
            "proj_w_words": words,
            "proj_w_scales": scales,
            "proj_b": bf(np.random.standard_normal(D) * 0.2)}


def core(attn, v, proj_w_words, proj_w_scales, proj_b):
    o = mxq(f64(attn), 4, "e4m3") @ mxq(f64(v), 3, "e4m3")
    o = o.transpose(0, 3, 2, 1, 4).reshape(B, -1, H * HD)
    return (mxq(o, 2, "e4m3") @ unpack4(proj_w_words, proj_w_scales)) + f64(proj_b)


def e4m3fn_bytes(y):
    return np.clip(np.asarray(y, np.float64), -448.0, 448.0).astype(np.float32).astype(ml_dtypes.float8_e4m3fn).view(np.uint8)


def e4m3fn_values(b):
    return np.asarray(b, np.uint8).view(ml_dtypes.float8_e4m3fn).astype(np.float64)


def setup_inputs():
    d = draw0()
    x0 = np.asarray(d['attn']).astype(np.float64)
    s = (np.max(np.abs(x0), axis=(0, 1, 2, 3), keepdims=True) / 448.0).astype(np.float32)
    out = {}
    for k, v in d.items():
        if k == 'attn':
            out['attn_bytes'] = e4m3fn_bytes(x0 / s.astype(np.float64))
            out['attn_scale'] = s
        else:
            out[k] = v
    return out


def reference(attn_bytes, attn_scale, v, proj_w_words, proj_w_scales, proj_b):
    return core(e4m3fn_values(attn_bytes) * attn_scale.astype(np.float64), v, proj_w_words, proj_w_scales, proj_b)

@@ -1,0 +1,279 @@
+from contextlib import ExitStack
+
+import concourse.mybir as mybir
+from concourse.masks import make_identity
+
+H, NWIN, NQ, SEQ, HD, D = 16, 3, 128, 512, 64, 1024
+
+FLOPS = 2 * H * NWIN * NQ * SEQ * HD + 2 * NWIN * NQ * D * D
+
+F32 = mybir.dt.float32
+BF16 = mybir.dt.bfloat16
+I32 = mybir.dt.int32
+U32 = mybir.dt.uint32
+U8 = mybir.dt.uint8
+FP8 = mybir.dt.float8_e4m3fn
+FP8X4 = mybir.dt.float8_e4m3fn_x4
+FP4X4 = mybir.dt.float4_e2m1fn_x4
+MULT = mybir.AluOpType.mult
+ADD = mybir.AluOpType.add
+
+P = 128
+UH = 4
+UPW = H // UH
+NU = NWIN * UPW
+
+
+def tile_hieramaskunitattention_pb_w4_kernel(tc, attn_bytes, attn_scale, v, w_words, w_scales, proj_b, out):
+    nc = tc.nc
+    with ExitStack() as ctx:
+        keep = ctx.enter_context(tc.tile_pool(name="keep", bufs=1))
+        rot = ctx.enter_context(tc.tile_pool(name="rot", bufs=3))
+        psum = ctx.enter_context(tc.psum_pool(name="psum", bufs=1))
+        ctx.enter_context(tc.manual_schedule())
+
+        ident = keep.tile([P, P], F32)
+        make_identity(nc, ident[:])
+        wsc = keep.tile([P, 2, D], U8, align_bytes=64)
+        nc.vector.memset(wsc[:].rearrange("p g n -> p (g n)").bitcast(I32), 0)
+
+        scale = keep.tile([P, 2, SEQ], F32, align_bytes=64)
+        nc.scalar.dma_start(out=scale[:, 0, :], in_=attn_scale.rearrange("a b c d k -> (a b c d k)").partition_broadcast(P))
+
+        ab = []
+        vraw = []
+        for u in range(NU):
+            ab.append(keep.tile([P, UH, SEQ], U8, name=f"ab{u}", align_bytes=64))
+            vraw.append(keep.tile([P, UH, 4 * HD], BF16, name=f"vraw{u}", align_bytes=64))
+
+        def load_v(u):
+            w, h0 = u // UPW, UH * (u % UPW)
+            nc.sync.dma_start(out=vraw[u][:], in_=v[0, h0 : h0 + UH, w].rearrange("h (p j) d -> p h (j d)", j=4))
+
+        def load_a(u, lo, hi):
+            w, h0 = u // UPW, UH * (u % UPW)
+            nc.sync.dma_start(out=ab[u][:, lo:hi, :], in_=attn_bytes[0, h0 + lo : h0 + hi, w].rearrange("h q k -> q h k"))
+
+        wt = keep.tile([P, 2, 2 * D], U8, align_bytes=64)
+        bias = keep.tile([P, D], BF16, align_bytes=64)
+        load_v(0)
+        load_a(0, 0, 1)
+        load_a(0, 1, 2)
+        load_a(0, 2, 4)
+        for u in range(1, NU):
+            load_v(u)
+            load_a(u, 0, UH)
+            if u == 3:
+                for g in range(2):
+                    nc.sync.dma_start(out=wt[:, g, :].bitcast(I32), in_=w_words[g].bitcast(I32))
+                for q in range(4):
+                    nc.sync.dma_start(
+                        out=wsc[32 * q : 32 * q + 4, :, :].bitcast(I32),
+                        in_=w_scales[:, 4 * q : 4 * q + 4, :].rearrange("g r n -> r g n").bitcast(I32),
+                    )
+                nc.sync.dma_start(out=bias[:], in_=proj_b.partition_broadcast(P))
+
+        prod = {}
+        tp = {}
+        grp = {}
+        acodes = {}
+        vgrp = {}
+        vcodes = {}
+        o_ps = {}
+        obf = {}
+        ot = {}
+        ogrp = {}
+        mcodes = {}
+        fin = {}
+        res = {}
+
+        def product(u, h0, n):
+            t = rot.tile([P, 2, SEQ], BF16, name="prod", align_bytes=64, bufs=4)
+            prod[u, h0] = t
+            nc.vector.tensor_tensor(
+                out=t[:, :n, :].rearrange("p h k -> p (h k)"),
+                in0=ab[u][:, h0 : h0 + n, :].rearrange("p h k -> p (h k)").bitcast(FP8),
+                in1=scale[:, :n, :].rearrange("p h k -> p (h k)"),
+                op=MULT,
+            )
+
+        def turn(u, h0, n):
+            words = prod[u, h0][:].rearrange("p h k -> p (h k)").bitcast(F32)
+            t = psum.tile([P, 2, 2, P], F32, name="tp", bufs=4)
+            tp[u, h0] = t
+            for h in range(n):
+                for e in range(2):
+                    nc.tensor.transpose(t[:, h, e, :], words[:, 256 * h + e : 256 * (h + 1) : 2], ident[:])
+
+        def empty(u, h0, n):
+            if h0 == 0:
+                grp[u] = rot.tile([P, UH, P, 2], F32, name="grp", align_bytes=64)
+            nc.scalar.copy(out=grp[u][:, h0 : h0 + n, :, :], in_=tp[u, h0][:, :n].rearrange("p h e r -> p h r e"))
+
+        def quant_attn(u, h0, n):
+            if h0 == 0:
+                c = rot.tile([P, UH * P], U32, name="ac", align_bytes=64)
+                s = rot.tile([P, UH * P], U8, name="asc", align_bytes=64)
+                acodes[u] = (c, s)
+            c, s = acodes[u]
+            cols = slice(P * h0, P * (h0 + n))
+            nc.vector.quantize_mx(
+                out=c[:, cols].bitcast(FP8X4),
+                scales=s[:, cols],
+                in_=grp[u][:, h0 : h0 + n].rearrange("p h r e -> p (h r e)").bitcast(BF16),
+            )
+
+        def inter_v(u, on_vector):
+            t = rot.tile([P, UH, HD, 4], BF16, name="vgrp", align_bytes=64)
+            vgrp[u] = t
+            src = vraw[u][:].rearrange("p h (j d) -> p h d j", j=4)
+            if on_vector:
+                nc.vector.tensor_copy(out=t[:], in_=src)
+            else:
+                nc.scalar.copy(out=t[:], in_=src)
+
+        def quant_v(u):
+            c = rot.tile([P, UH * HD], U32, name="vc", align_bytes=64, bufs=4)
+            s = rot.tile([P, UH * HD], U8, name="vsc", align_bytes=64, bufs=4)
+            vcodes[u] = (c, s)
+            nc.vector.quantize_mx(
+                out=c[:].bitcast(FP8X4), scales=s[:], in_=vgrp[u][:].rearrange("p h d j -> p (h d j)")
+            )
+
+        def mix(u, h0, n):
+            g = u // 2
+            if u % 2 == 0 and h0 == 0:
+                o_ps[g] = psum.tile([P, 8 * HD], F32, name="o_ps", bufs=1)
+            ac, asc = acodes[u]
+            vc, vsc = vcodes[u]
+            for h in range(h0, h0 + n):
+                hh = UH * (u % 2) + h
+                q = slice(P * h, P * (h + 1))
+                d = slice(HD * h, HD * (h + 1))
+                nc.tensor.matmul_mx(
+                    out=o_ps[g][:, HD * hh : HD * (hh + 1)],
+                    lhsT=ac[:, q].bitcast(FP8X4),
+                    lhsT_scale=asc[:, q],
+                    rhs=vc[:, d].bitcast(FP8X4),
+                    rhs_scale=vsc[:, d],
+                    start=True,
+                    stop=True,
+                )
+
+        def empty_o(g, h0, n):
+            if h0 == 0:
+                obf[g] = rot.tile([P, 8 * HD], BF16, name="obf", align_bytes=64, bufs=2)
+            cols = slice(HD * h0, HD * (h0 + n))
+            nc.scalar.copy(out=obf[g][:, cols], in_=o_ps[g][:, cols])
+
+        def turn_o(g):
+            t = psum.tile([P, 2, P], F32, name="ot", bufs=1)
+            ot[g] = t
+            words = obf[g][:].bitcast(F32)
+            for e in range(2):
+                nc.tensor.transpose(t[:, e, :], words[:, e::2], ident[:])
+
+        def empty_ot(g):
+            t = rot.tile([P, P, 2], F32, name="ogrp", align_bytes=64, bufs=2)
+            ogrp[g] = t
+            nc.scalar.copy(out=t[:], in_=ot[g][:].rearrange("p e r -> p r e"))
+
+        def quant_o(g):
+            c = rot.tile([P, P], U32, name="mc", align_bytes=64)
+            s = rot.tile([P, P], U8, name="msc", align_bytes=64)
+            mcodes[g] = (c, s)
+            nc.vector.quantize_mx(
+                out=c[:].bitcast(FP8X4), scales=s[:], in_=ogrp[g][:].rearrange("p r e -> p (r e)").bitcast(BF16)
+            )
+
+        def project(g):
+            w, gg = g // 2, g % 2
+            c, s = mcodes[g]
+            for n in range(2):
+                if gg == 0:
+                    fin[w, n] = psum.tile([P, 512], F32, name=f"fin{n}", bufs=1)
+                nc.tensor.matmul_mx(
+                    out=fin[w, n][:],
+                    lhsT=c[:].bitcast(FP8X4),
+                    lhsT_scale=s[:],
+                    rhs=wt[:, gg, 1024 * n : 1024 * (n + 1)].bitcast(FP4X4),
+                    rhs_scale=wsc[:, gg, 512 * n : 512 * (n + 1)],
+                    start=(gg == 0),
+                    stop=(gg == 1),
+                )
+
+        out_w = out[0].rearrange("(i w) n -> w i n", w=NWIN)
+
+        def copy_fin(w, n):
+            t = rot.tile([P, 512], F32, name=f"raw{w}{n}", align_bytes=64, bufs=1)
+            fin[w, n, "sb"] = t
+            nc.scalar.copy(out=t[:], in_=fin[w, n][:])
+
+        def finish(w, n):
+            cols = slice(512 * n, 512 * (n + 1))
+            t = rot.tile([P, 512], F32, name=f"res{w}{n}", align_bytes=64, bufs=1)
+            src = fin[w, n, "sb"] if w < 2 else fin[w, n]
+            nc.vector.tensor_tensor(out=t[:], in0=src[:], in1=bias[:, cols], op=ADD)
+            nc.sync.dma_start(out=out_w[w, :, cols], in_=t[:])
+
+        inter_v(0, True)
+        nc.scalar.copy(out=scale[:, 1, :], in_=scale[:, 0, :])
+        for s in range(NU):
+            g = (s - 3) // 2 if s % 2 == 1 and s >= 3 else None
+            gp = (s - 4) // 2 if s % 2 == 0 and s >= 4 else None
+            if gp is not None:
+                project(gp)
+            if g is not None:
+                empty_o(g, 0, 8)
+                turn_o(g)
+            if s + 1 < NU:
+                inter_v(s + 1, False)
+            first = [(0, 1), (1, 1)] if s == 0 else [(0, 2)]
+            second = [(2, 1), (3, 1)] if s == NU - 1 else [(2, 2)]
+            for h0, n in first:
+                product(s, h0, n)
+                turn(s, h0, n)
+            if s == 0:
+                quant_v(0)
+            for h0, n in second:
+                product(s, h0, n)
+                turn(s, h0, n)
+            for h0, n in first:
+                empty(s, h0, n)
+            if g is not None:
+                empty_ot(g)
+            if gp is not None and gp % 2 == 1:
+                copy_fin(gp // 2, 0)
+            for h0, n in second:
+                empty(s, h0, n)
+            if gp is not None and gp % 2 == 1:
+                copy_fin(gp // 2, 1)
+            if s >= 1:
+                quant_attn(s - 1, 0, UH)
+                mix(s - 1, 0, UH)
+            if s + 1 < NU:
+                quant_v(s + 1)
+            if g is not None:
+                quant_o(g)
+
+        u, g = NU - 1, NU // 2 - 1
+        project(g - 1)
+        empty_o(g, 0, 4)
+        quant_attn(u, 0, 2)
+        mix(u, 0, 2)
+        finish(0, 0)
+        quant_attn(u, 2, 1)
+        mix(u, 2, 1)
+        quant_attn(u, 3, 1)
+        mix(u, 3, 1)
+        empty_o(g, 4, 2)
+        empty_o(g, 6, 2)
+        finish(0, 1)
+        turn_o(g)
+        empty_ot(g)
+        finish(1, 0)
+        quant_o(g)
+        project(g)
+        finish(1, 1)
+        finish(2, 0)
+        finish(2, 1)

@@ -37,8 +37,10 @@ def tile_hieramaskunitattention_pb_w4_kernel(tc, attn_bytes, attn_scale, v, w_wo
         wsc = keep.tile([P, 2, D], U8, align_bytes=64)
         nc.vector.memset(wsc[:].rearrange("p g n -> p (g n)").bitcast(I32), 0)
 
-        scale = keep.tile([P, 2, SEQ], F32, align_bytes=64)
-        nc.scalar.dma_start(out=scale[:, 0, :], in_=attn_scale.rearrange("a b c d k -> (a b c d k)").partition_broadcast(P))
+        scale = keep.tile([P, 1, 2, 2], F32, align_bytes=64)
+        nc.scalar.dma_start(
+            out=scale[:].rearrange("p o u e -> p (o u e)"), in_=attn_scale.rearrange("a b c d (p t) -> p (a b c d t)", t=4)
+        )
 
         ab = []
         vraw = []
@@ -56,13 +58,12 @@ def tile_hieramaskunitattention_pb_w4_kernel(tc, attn_bytes, attn_scale, v, w_wo
 
         wt = keep.tile([P, 2, 2 * D], U8, align_bytes=64)
         bias = keep.tile([P, D], BF16, align_bytes=64)
-        load_v(0)
-        load_a(0, 0, 1)
-        load_a(0, 1, 2)
+        load_a(0, 0, 2)
         load_a(0, 2, 4)
+        load_v(0)
         for u in range(1, NU):
-            load_v(u)
             load_a(u, 0, UH)
+            load_v(u)
             if u == 3:
                 for g in range(2):
                     nc.sync.dma_start(out=wt[:, g, :].bitcast(I32), in_=w_words[g].bitcast(I32))
@@ -73,7 +74,7 @@ def tile_hieramaskunitattention_pb_w4_kernel(tc, attn_bytes, attn_scale, v, w_wo
                     )
                 nc.sync.dma_start(out=bias[:], in_=proj_b.partition_broadcast(P))
 
-        prod = {}
+        wide = {}
         tp = {}
         grp = {}
         acodes = {}
@@ -87,28 +88,36 @@ def tile_hieramaskunitattention_pb_w4_kernel(tc, attn_bytes, attn_scale, v, w_wo
         fin = {}
         res = {}
 
+        def widen(u, half, on_vector):
+            if half == 0:
+                wide[u] = rot.tile([P, UH, SEQ], BF16, name="wide", align_bytes=64, bufs=4)
+            dst = wide[u][:, 2 * half : 2 * half + 2, :].rearrange("p h k -> p (h k)")
+            src = ab[u][:, 2 * half : 2 * half + 2, :].rearrange("p h k -> p (h k)").bitcast(FP8)
+            if on_vector:
+                nc.vector.tensor_copy(out=dst, in_=src)
+            else:
+                nc.scalar.copy(out=dst, in_=src)
+
+        def turn(u, half):
+            words = wide[u][:].rearrange("p h k -> p (h k)").bitcast(F32)
+            t = psum.tile([P, 2, 2, P], F32, name="tp", bufs=4)
+            tp[u, half] = t
+            for i in range(2):
+                h = 2 * half + i
+                for e in range(2):
+                    nc.tensor.transpose(t[:, e, i, :], words[:, 256 * h + e : 256 * (h + 1) : 2], ident[:])
+
         def product(u, h0, n):
-            t = rot.tile([P, 2, SEQ], BF16, name="prod", align_bytes=64, bufs=4)
-            prod[u, h0] = t
+            if h0 == 0:
+                grp[u] = rot.tile([P, UH * P, 2, 2], BF16, name="grp", align_bytes=64)
+            half, i = h0 // 2, h0 % 2
+            src = tp[u, half][:].rearrange("p u h r -> p u (h r)").bitcast(BF16).rearrange("p u (r e) -> p r u e", e=2)
             nc.vector.tensor_tensor(
-                out=t[:, :n, :].rearrange("p h k -> p (h k)"),
-                in0=ab[u][:, h0 : h0 + n, :].rearrange("p h k -> p (h k)").bitcast(FP8),
-                in1=scale[:, :n, :].rearrange("p h k -> p (h k)"),
+                out=grp[u][:, P * h0 : P * (h0 + n)],
+                in0=src[:, P * i : P * (i + n)],
+                in1=scale[:].to_broadcast([P, P * n, 2, 2]),
                 op=MULT,
             )
-
-        def turn(u, h0, n):
-            words = prod[u, h0][:].rearrange("p h k -> p (h k)").bitcast(F32)
-            t = psum.tile([P, 2, 2, P], F32, name="tp", bufs=4)
-            tp[u, h0] = t
-            for h in range(n):
-                for e in range(2):
-                    nc.tensor.transpose(t[:, h, e, :], words[:, 256 * h + e : 256 * (h + 1) : 2], ident[:])
-
-        def empty(u, h0, n):
-            if h0 == 0:
-                grp[u] = rot.tile([P, UH, P, 2], F32, name="grp", align_bytes=64)
-            nc.scalar.copy(out=grp[u][:, h0 : h0 + n, :, :], in_=tp[u, h0][:, :n].rearrange("p h e r -> p h r e"))
 
         def quant_attn(u, h0, n):
             if h0 == 0:
@@ -120,7 +129,7 @@ def tile_hieramaskunitattention_pb_w4_kernel(tc, attn_bytes, attn_scale, v, w_wo
             nc.vector.quantize_mx(
                 out=c[:, cols].bitcast(FP8X4),
                 scales=s[:, cols],
-                in_=grp[u][:, h0 : h0 + n].rearrange("p h r e -> p (h r e)").bitcast(BF16),
+                in_=grp[u][:, P * h0 : P * (h0 + n)].rearrange("p r u e -> p (r u e)"),
             )
 
         def inter_v(u, on_vector):
@@ -130,7 +139,7 @@ def tile_hieramaskunitattention_pb_w4_kernel(tc, attn_bytes, attn_scale, v, w_wo
             if on_vector:
                 nc.vector.tensor_copy(out=t[:], in_=src)
             else:
-                nc.scalar.copy(out=t[:], in_=src)
+                nc.gpsimd.tensor_scalar(out=t[:], in0=src, scalar1=1.0, scalar2=0.0, op0=MULT, op1=ADD)
 
         def quant_v(u):
             c = rot.tile([P, UH * HD], U32, name="vc", align_bytes=64, bufs=4)
@@ -216,8 +225,14 @@ def tile_hieramaskunitattention_pb_w4_kernel(tc, attn_bytes, attn_scale, v, w_wo
             nc.vector.tensor_tensor(out=t[:], in0=src[:], in1=bias[:, cols], op=ADD)
             nc.sync.dma_start(out=out_w[w, :, cols], in_=t[:])
 
+        widen(0, 0, True)
+        turn(0, 0)
+        widen(0, 1, False)
+        turn(0, 1)
         inter_v(0, True)
-        nc.scalar.copy(out=scale[:, 1, :], in_=scale[:, 0, :])
+        inter_v(1, False)
+        widen(1, 0, False)
+        widen(1, 1, False)
         for s in range(NU):
             g = (s - 3) // 2 if s % 2 == 1 and s >= 3 else None
             gp = (s - 4) // 2 if s % 2 == 0 and s >= 4 else None
@@ -227,47 +242,45 @@ def tile_hieramaskunitattention_pb_w4_kernel(tc, attn_bytes, attn_scale, v, w_wo
                 empty_o(g, 0, 8)
                 turn_o(g)
             if s + 1 < NU:
-                inter_v(s + 1, False)
-            first = [(0, 1), (1, 1)] if s == 0 else [(0, 2)]
-            second = [(2, 1), (3, 1)] if s == NU - 1 else [(2, 2)]
-            for h0, n in first:
-                product(s, h0, n)
-                turn(s, h0, n)
-            if s == 0:
-                quant_v(0)
-            for h0, n in second:
-                product(s, h0, n)
-                turn(s, h0, n)
-            for h0, n in first:
-                empty(s, h0, n)
+                turn(s + 1, 0)
+                turn(s + 1, 1)
+            if s + 2 < NU:
+                inter_v(s + 2, False)
+                widen(s + 2, 0, False)
             if g is not None:
                 empty_ot(g)
             if gp is not None and gp % 2 == 1:
                 copy_fin(gp // 2, 0)
-            for h0, n in second:
-                empty(s, h0, n)
-            if gp is not None and gp % 2 == 1:
                 copy_fin(gp // 2, 1)
-            if s >= 1:
+            if s + 2 < NU:
+                widen(s + 2, 1, False)
+            product(s, 0, 2)
+            if s == 0:
+                quant_v(0)
+            else:
                 quant_attn(s - 1, 0, UH)
                 mix(s - 1, 0, UH)
-            if s + 1 < NU:
+            if s < NU - 1:
+                product(s, 2, 2)
                 quant_v(s + 1)
-            if g is not None:
-                quant_o(g)
+                if g is not None:
+                    quant_o(g)
 
         u, g = NU - 1, NU // 2 - 1
-        project(g - 1)
-        empty_o(g, 0, 4)
+        quant_o(g - 1)
+        product(u, 2, 1)
         quant_attn(u, 0, 2)
+        project(g - 1)
         mix(u, 0, 2)
-        finish(0, 0)
+        product(u, 3, 1)
         quant_attn(u, 2, 1)
         mix(u, 2, 1)
         quant_attn(u, 3, 1)
         mix(u, 3, 1)
+        empty_o(g, 0, 4)
         empty_o(g, 4, 2)
         empty_o(g, 6, 2)
+        finish(0, 0)
         finish(0, 1)
         turn_o(g)
         empty_ot(g)

@@ -58,13 +58,14 @@ def tile_hieramaskunitattention_pb_w4_kernel(tc, attn_bytes, attn_scale, v, w_wo
 
         wt = keep.tile([P, 2, 2 * D], U8, align_bytes=64)
         bias = keep.tile([P, D], BF16, align_bytes=64)
-        load_a(0, 0, 2)
+        load_a(0, 0, 1)
+        load_a(0, 1, 2)
         load_a(0, 2, 4)
         load_v(0)
         for u in range(1, NU):
             load_a(u, 0, UH)
             load_v(u)
-            if u == 3:
+            if u == 5:
                 for g in range(2):
                     nc.sync.dma_start(out=wt[:, g, :].bitcast(I32), in_=w_words[g].bitcast(I32))
                 for q in range(4):
@@ -72,7 +73,8 @@ def tile_hieramaskunitattention_pb_w4_kernel(tc, attn_bytes, attn_scale, v, w_wo
                         out=wsc[32 * q : 32 * q + 4, :, :].bitcast(I32),
                         in_=w_scales[:, 4 * q : 4 * q + 4, :].rearrange("g r n -> r g n").bitcast(I32),
                     )
-                nc.sync.dma_start(out=bias[:], in_=proj_b.partition_broadcast(P))
+
+        nc.sync.dma_start(out=bias[:], in_=proj_b.partition_broadcast(P))
 
         wide = {}
         tp = {}
@@ -88,33 +90,32 @@ def tile_hieramaskunitattention_pb_w4_kernel(tc, attn_bytes, attn_scale, v, w_wo
         fin = {}
         res = {}
 
-        def widen(u, half, on_vector):
-            if half == 0:
+        def widen(u, h0, n, on_vector=False):
+            if h0 == 0:
                 wide[u] = rot.tile([P, UH, SEQ], BF16, name="wide", align_bytes=64, bufs=4)
-            dst = wide[u][:, 2 * half : 2 * half + 2, :].rearrange("p h k -> p (h k)")
-            src = ab[u][:, 2 * half : 2 * half + 2, :].rearrange("p h k -> p (h k)").bitcast(FP8)
+            dst = wide[u][:, h0 : h0 + n, :].rearrange("p h k -> p (h k)")
+            src = ab[u][:, h0 : h0 + n, :].rearrange("p h k -> p (h k)").bitcast(FP8)
             if on_vector:
                 nc.vector.tensor_copy(out=dst, in_=src)
             else:
                 nc.scalar.copy(out=dst, in_=src)
 
-        def turn(u, half):
+        def turn(u, h0, n):
             words = wide[u][:].rearrange("p h k -> p (h k)").bitcast(F32)
             t = psum.tile([P, 2, 2, P], F32, name="tp", bufs=4)
-            tp[u, half] = t
-            for i in range(2):
-                h = 2 * half + i
+            tp[u, h0] = t
+            for i in range(n):
+                h = h0 + i
                 for e in range(2):
                     nc.tensor.transpose(t[:, e, i, :], words[:, 256 * h + e : 256 * (h + 1) : 2], ident[:])
 
         def product(u, h0, n):
             if h0 == 0:
                 grp[u] = rot.tile([P, UH * P, 2, 2], BF16, name="grp", align_bytes=64)
-            half, i = h0 // 2, h0 % 2
-            src = tp[u, half][:].rearrange("p u h r -> p u (h r)").bitcast(BF16).rearrange("p u (r e) -> p r u e", e=2)
+            src = tp[u, h0][:].rearrange("p u h r -> p u (h r)").bitcast(BF16).rearrange("p u (r e) -> p r u e", e=2)
             nc.vector.tensor_tensor(
                 out=grp[u][:, P * h0 : P * (h0 + n)],
-                in0=src[:, P * i : P * (i + n)],
+                in0=src[:, : P * n],
                 in1=scale[:].to_broadcast([P, P * n, 2, 2]),
                 op=MULT,
             )
@@ -132,12 +133,14 @@ def tile_hieramaskunitattention_pb_w4_kernel(tc, attn_bytes, attn_scale, v, w_wo
                 in_=grp[u][:, P * h0 : P * (h0 + n)].rearrange("p r u e -> p (r u e)"),
             )
 
-        def inter_v(u, on_vector):
-            t = rot.tile([P, UH, HD, 4], BF16, name="vgrp", align_bytes=64)
+        def inter_v(u, engine):
+            t = rot.tile([P, UH, HD, 4], BF16, name="vgrp", align_bytes=64, bufs=2)
             vgrp[u] = t
             src = vraw[u][:].rearrange("p h (j d) -> p h d j", j=4)
-            if on_vector:
+            if engine == "vector":
                 nc.vector.tensor_copy(out=t[:], in_=src)
+            elif engine == "scalar":
+                nc.scalar.copy(out=t[:], in_=src)
             else:
                 nc.gpsimd.tensor_scalar(out=t[:], in0=src, scalar1=1.0, scalar2=0.0, op0=MULT, op1=ADD)
 
@@ -225,49 +228,57 @@ def tile_hieramaskunitattention_pb_w4_kernel(tc, attn_bytes, attn_scale, v, w_wo
             nc.vector.tensor_tensor(out=t[:], in0=src[:], in1=bias[:, cols], op=ADD)
             nc.sync.dma_start(out=out_w[w, :, cols], in_=t[:])
 
-        widen(0, 0, True)
-        turn(0, 0)
-        widen(0, 1, False)
-        turn(0, 1)
-        inter_v(0, True)
-        inter_v(1, False)
-        widen(1, 0, False)
-        widen(1, 1, False)
+        def pieces(u):
+            return [(2, 1), (3, 1)] if u == NU - 1 else [(2, 2)]
+
+        widen(0, 0, 1, True)
+        turn(0, 0, 1)
+        widen(0, 1, 1)
+        turn(0, 1, 1)
+        widen(0, 2, 2)
+        turn(0, 2, 2)
+        inter_v(0, "gpsimd")
+        widen(1, 0, 2)
+        widen(1, 2, 2)
         for s in range(NU):
             g = (s - 3) // 2 if s % 2 == 1 and s >= 3 else None
             gp = (s - 4) // 2 if s % 2 == 0 and s >= 4 else None
+            if g is not None:
+                empty_o(g, 0, 8)
+            if s + 1 < NU:
+                turn(s + 1, 0, 2)
+                for h0, n in pieces(s + 1):
+                    turn(s + 1, h0, n)
             if gp is not None:
                 project(gp)
             if g is not None:
-                empty_o(g, 0, 8)
                 turn_o(g)
-            if s + 1 < NU:
-                turn(s + 1, 0)
-                turn(s + 1, 1)
             if s + 2 < NU:
-                inter_v(s + 2, False)
-                widen(s + 2, 0, False)
+                widen(s + 2, 0, 2)
             if g is not None:
                 empty_ot(g)
             if gp is not None and gp % 2 == 1:
                 copy_fin(gp // 2, 0)
                 copy_fin(gp // 2, 1)
             if s + 2 < NU:
-                widen(s + 2, 1, False)
-            product(s, 0, 2)
+                widen(s + 2, 2, 2)
+            if s + 1 < NU:
+                inter_v(s + 1, "gpsimd")
             if s == 0:
-                quant_v(0)
+                product(0, 0, 1)
+                product(0, 1, 1)
             else:
-                quant_attn(s - 1, 0, UH)
-                mix(s - 1, 0, UH)
+                product(s, 0, 2)
             if s < NU - 1:
                 product(s, 2, 2)
-                quant_v(s + 1)
-                if g is not None:
-                    quant_o(g)
+            if s > 0:
+                quant_attn(s - 1, 0, UH)
+                mix(s - 1, 0, UH)
+            if g is not None:
+                quant_o(g)
+            quant_v(s)
 
         u, g = NU - 1, NU // 2 - 1
-        quant_o(g - 1)
         product(u, 2, 1)
         quant_attn(u, 0, 2)
         project(g - 1)

@@ -17,6 +17,8 @@ FP8X4 = mybir.dt.float8_e4m3fn_x4
 FP4X4 = mybir.dt.float4_e2m1fn_x4
 MULT = mybir.AluOpType.mult
 ADD = mybir.AluOpType.add
+COPY = mybir.ActivationFunctionType.Copy
+SPLIT = {}
 
 P = 128
 UH = 4
@@ -61,11 +63,13 @@ def tile_hieramaskunitattention_pb_w4_kernel(tc, attn_bytes, attn_scale, v, w_wo
         load_a(0, 0, 1)
         load_a(0, 1, 2)
         load_a(0, 2, 4)
+        load_a(1, 0, UH)
         load_v(0)
-        for u in range(1, NU):
+        load_v(1)
+        for u in range(2, NU):
             load_a(u, 0, UH)
             load_v(u)
-            if u == 5:
+            if u == 7:
                 for g in range(2):
                     nc.sync.dma_start(out=wt[:, g, :].bitcast(I32), in_=w_words[g].bitcast(I32))
                 for q in range(4):
@@ -109,9 +113,12 @@ def tile_hieramaskunitattention_pb_w4_kernel(tc, attn_bytes, attn_scale, v, w_wo
                 for e in range(2):
                     nc.tensor.transpose(t[:, e, i, :], words[:, 256 * h + e : 256 * (h + 1) : 2], ident[:])
 
-        def product(u, h0, n):
-            if h0 == 0:
+        def group_tile(u):
+            if u not in grp:
                 grp[u] = rot.tile([P, UH * P, 2, 2], BF16, name="grp", align_bytes=64)
+
+        def product(u, h0, n):
+            group_tile(u)
             src = tp[u, h0][:].rearrange("p u h r -> p u (h r)").bitcast(BF16).rearrange("p u (r e) -> p r u e", e=2)
             nc.vector.tensor_tensor(
                 out=grp[u][:, P * h0 : P * (h0 + n)],
@@ -119,6 +126,26 @@ def tile_hieramaskunitattention_pb_w4_kernel(tc, attn_bytes, attn_scale, v, w_wo
                 in1=scale[:].to_broadcast([P, P * n, 2, 2]),
                 op=MULT,
             )
+
+        def product_planes(u, h0, n, engine):
+            group_tile(u)
+            t = rot.tile([P, 4, P * n], BF16, name="planes", align_bytes=64)
+            src = tp[u, h0][:].rearrange("p u h r -> p u (h r)").bitcast(BF16).rearrange("p u (r e) -> p u e r", e=2)
+            for j in range(4):
+                nc.scalar.activation(
+                    out=t[:, j, :],
+                    in_=src[:, j // 2, j % 2, : P * n],
+                    func=COPY,
+                    scale=scale[:, 0, j // 2, j % 2 : j % 2 + 1],
+                )
+            dst = grp[u][:, P * h0 : P * (h0 + n)].rearrange("p r u e -> p r (u e)")
+            pl = t[:].rearrange("p j r -> p r j")
+            if engine == "scalar":
+                nc.scalar.copy(out=dst, in_=pl)
+            elif engine == "vector":
+                nc.vector.tensor_copy(out=dst, in_=pl)
+            else:
+                nc.gpsimd.tensor_scalar(out=dst, in0=pl, scalar1=1.0, scalar2=0.0, op0=MULT, op1=ADD)
 
         def quant_attn(u, h0, n):
             if h0 == 0:
@@ -134,7 +161,7 @@ def tile_hieramaskunitattention_pb_w4_kernel(tc, attn_bytes, attn_scale, v, w_wo
             )
 
         def inter_v(u, engine):
-            t = rot.tile([P, UH, HD, 4], BF16, name="vgrp", align_bytes=64, bufs=2)
+            t = rot.tile([P, UH, HD, 4], BF16, name="vgrp" if engine == "gpsimd" else "vgrp_last", align_bytes=64, bufs=2)
             vgrp[u] = t
             src = vraw[u][:].rearrange("p h (j d) -> p h d j", j=4)
             if engine == "vector":
@@ -203,7 +230,10 @@ def tile_hieramaskunitattention_pb_w4_kernel(tc, attn_bytes, attn_scale, v, w_wo
             c, s = mcodes[g]
             for n in range(2):
                 if gg == 0:
-                    fin[w, n] = psum.tile([P, 512], F32, name=f"fin{n}", bufs=1)
+                    if w < 2:
+                        fin[w, n] = psum.tile([P, 512], F32, name=f"fin{n}", bufs=1)
+                    else:
+                        fin[w, n] = psum.tile([P, 512], F32, name="tp", bufs=4)
                 nc.tensor.matmul_mx(
                     out=fin[w, n][:],
                     lhsT=c[:].bitcast(FP8X4),
@@ -224,62 +254,74 @@ def tile_hieramaskunitattention_pb_w4_kernel(tc, attn_bytes, attn_scale, v, w_wo
         def finish(w, n):
             cols = slice(512 * n, 512 * (n + 1))
             t = rot.tile([P, 512], F32, name=f"res{w}{n}", align_bytes=64, bufs=1)
-            src = fin[w, n, "sb"] if w < 2 else fin[w, n]
+            src = fin[w, n, "sb"] if w == 0 else fin[w, n]
             nc.vector.tensor_tensor(out=t[:], in0=src[:], in1=bias[:, cols], op=ADD)
             nc.sync.dma_start(out=out_w[w, :, cols], in_=t[:])
 
         def pieces(u):
-            return [(2, 1), (3, 1)] if u == NU - 1 else [(2, 2)]
+            if u in SPLIT:
+                return SPLIT[u]
+            if u == 0:
+                return [(0, 1, "v"), (1, 1, "v"), (2, 2, "v")]
+            if u == NU - 1:
+                return [(0, 2, "v"), (2, 1, "v"), (3, 1, "v")]
+            return [(0, 2, "v"), (2, 2, "v")]
 
         widen(0, 0, 1, True)
-        turn(0, 0, 1)
         widen(0, 1, 1)
+        turn(0, 0, 1)
         turn(0, 1, 1)
-        widen(0, 2, 2)
+        widen(0, 2, 1, True)
+        widen(0, 3, 1)
         turn(0, 2, 2)
         inter_v(0, "gpsimd")
+        inter_v(1, "gpsimd")
         widen(1, 0, 2)
         widen(1, 2, 2)
         for s in range(NU):
-            g = (s - 3) // 2 if s % 2 == 1 and s >= 3 else None
-            gp = (s - 4) // 2 if s % 2 == 0 and s >= 4 else None
-            if g is not None:
-                empty_o(g, 0, 8)
+            odd = s % 2 == 1
+            g = (s - 3) // 2 if odd and s >= 3 else None
+            gq = (s - 4) // 2 if not odd and s >= 4 else None
+            gp = {6: 0, 7: 1, 9: 2, 11: 3}.get(s)
             if s + 1 < NU:
-                turn(s + 1, 0, 2)
-                for h0, n in pieces(s + 1):
+                for h0, n, e in pieces(s + 1):
                     turn(s + 1, h0, n)
+            if s + 2 < NU:
+                widen(s + 2, 0, 2)
             if gp is not None:
                 project(gp)
             if g is not None:
+                empty_o(g, 0, 8)
                 turn_o(g)
             if s + 2 < NU:
-                widen(s + 2, 0, 2)
+                widen(s + 2, 2, 2)
+            for h0, n, e in pieces(s):
+                if e != "v":
+                    product_planes(s, h0, n, e)
             if g is not None:
                 empty_ot(g)
-            if gp is not None and gp % 2 == 1:
-                copy_fin(gp // 2, 0)
-                copy_fin(gp // 2, 1)
-            if s + 2 < NU:
-                widen(s + 2, 2, 2)
-            if s + 1 < NU:
-                inter_v(s + 1, "gpsimd")
-            if s == 0:
-                product(0, 0, 1)
-                product(0, 1, 1)
-            else:
-                product(s, 0, 2)
-            if s < NU - 1:
-                product(s, 2, 2)
+            if gp == 1:
+                copy_fin(0, 0)
+                copy_fin(0, 1)
+            if s == NU - 2:
+                inter_v(NU - 1, "scalar")
+            for h0, n, e in pieces(s):
+                if e == "v" and (s < NU - 1 or h0 == 0):
+                    product(s, h0, n)
+            if gq is not None:
+                quant_o(gq)
             if s > 0:
                 quant_attn(s - 1, 0, UH)
+                quant_v(s - 1)
                 mix(s - 1, 0, UH)
-            if g is not None:
-                quant_o(g)
-            quant_v(s)
+            if s + 2 < NU - 1:
+                inter_v(s + 2, "gpsimd")
 
         u, g = NU - 1, NU // 2 - 1
-        product(u, 2, 1)
+        if pieces(u)[1][2] == "v":
+            product(u, 2, 1)
+        quant_o(g - 1)
+        quant_v(u)
         quant_attn(u, 0, 2)
         project(g - 1)
         mix(u, 0, 2)

@@ -3,9 +3,9 @@ from contextlib import ExitStack
 import concourse.mybir as mybir
 from concourse.masks import make_identity
 
-H, NWIN, NQ, SEQ, HD, D = 16, 3, 128, 512, 64, 1024
+HEADS, WINDOWS, QUERIES, KEYS, HEAD_DIM, CHANNELS = 16, 3, 128, 512, 64, 1024
 
-FLOPS = 2 * H * NWIN * NQ * SEQ * HD + 2 * NWIN * NQ * D * D
+FLOPS = 2 * HEADS * WINDOWS * QUERIES * KEYS * HEAD_DIM + 2 * WINDOWS * QUERIES * CHANNELS * CHANNELS
 
 F32 = mybir.dt.float32
 BF16 = mybir.dt.bfloat16
@@ -18,328 +18,348 @@ FP4X4 = mybir.dt.float4_e2m1fn_x4
 MULT = mybir.AluOpType.mult
 ADD = mybir.AluOpType.add
 COPY = mybir.ActivationFunctionType.Copy
-SPLIT = {}
 
 P = 128
-UH = 4
-UPW = H // UH
-NU = NWIN * UPW
+PACK = 4
+BANK = 512
+
+UNIT_HEADS = 4
+GROUP_HEADS = 8
+UNITS = WINDOWS * HEADS // UNIT_HEADS
+GROUPS = UNITS // 2
+LAST = UNITS - 1
+
+PIECES = {0: ((0, 1), (1, 1), (2, 2)), LAST: ((0, 2), (2, 1), (3, 1))}
+USUAL_PIECES = ((0, 2), (2, 2))
+SHARED_UNITS = (5, 10)
+SHARED_PIECES = ((0, 2), (2, 1), (3, 1))
+WEIGHTS_BEHIND_UNIT = 7
+PROJECT_IN_STEP = {6: 0, 7: 1, 9: 2, 11: 3}
 
 
-def tile_hieramaskunitattention_pb_w4_kernel(tc, attn_bytes, attn_scale, v, w_words, w_scales, proj_b, out):
+def pieces(u):
+    if u in SHARED_UNITS:
+        return SHARED_PIECES
+    return PIECES.get(u, USUAL_PIECES)
+
+
+def on_scalar(u, h0):
+    return u in SHARED_UNITS and h0 == UNIT_HEADS - 1
+
+
+def tile_hieramaskunitattention_pb_w4_kernel(
+    tc, attn_bytes, attn_scale, v, proj_w_words, proj_w_scales, proj_b, out
+):
     nc = tc.nc
     with ExitStack() as ctx:
         keep = ctx.enter_context(tc.tile_pool(name="keep", bufs=1))
-        rot = ctx.enter_context(tc.tile_pool(name="rot", bufs=3))
+        work = ctx.enter_context(tc.tile_pool(name="work", bufs=3))
         psum = ctx.enter_context(tc.psum_pool(name="psum", bufs=1))
         ctx.enter_context(tc.manual_schedule())
 
-        ident = keep.tile([P, P], F32)
-        make_identity(nc, ident[:])
-        wsc = keep.tile([P, 2, D], U8, align_bytes=64)
-        nc.vector.memset(wsc[:].rearrange("p g n -> p (g n)").bitcast(I32), 0)
+        identity = keep.tile([P, P], F32)
+        make_identity(nc, identity[:])
 
-        scale = keep.tile([P, 1, 2, 2], F32, align_bytes=64)
+        w_scales = keep.tile([P, 2, CHANNELS], U8, align_bytes=64)
+        nc.vector.memset(w_scales[:].rearrange("p g n -> p (g n)").bitcast(I32), 0)
+
+        key_scale = keep.tile([P, 1, 2, 2], F32, align_bytes=64)
         nc.scalar.dma_start(
-            out=scale[:].rearrange("p o u e -> p (o u e)"), in_=attn_scale.rearrange("a b c d (p t) -> p (a b c d t)", t=4)
+            out=key_scale[:].rearrange("p o u e -> p (o u e)"),
+            in_=attn_scale.rearrange("a b c d (p t) -> p (a b c d t)", t=PACK),
         )
 
-        ab = []
-        vraw = []
-        for u in range(NU):
-            ab.append(keep.tile([P, UH, SEQ], U8, name=f"ab{u}", align_bytes=64))
-            vraw.append(keep.tile([P, UH, 4 * HD], BF16, name=f"vraw{u}", align_bytes=64))
+        codes_in = []
+        v_rows = []
+        for u in range(UNITS):
+            codes_in.append(keep.tile([P, UNIT_HEADS, KEYS], U8, name=f"codes_in{u}", align_bytes=64))
+            v_rows.append(keep.tile([P, UNIT_HEADS, PACK * HEAD_DIM], BF16, name=f"v_rows{u}", align_bytes=64))
+
+        def load_attn(u, h0, n):
+            w, first = u // 4, UNIT_HEADS * (u % 4) + h0
+            nc.sync.dma_start(
+                out=codes_in[u][:, h0 : h0 + n, :],
+                in_=attn_bytes[0, first : first + n, w].rearrange("h q k -> q h k"),
+            )
 
         def load_v(u):
-            w, h0 = u // UPW, UH * (u % UPW)
-            nc.sync.dma_start(out=vraw[u][:], in_=v[0, h0 : h0 + UH, w].rearrange("h (p j) d -> p h (j d)", j=4))
+            w, first = u // 4, UNIT_HEADS * (u % 4)
+            nc.sync.dma_start(
+                out=v_rows[u][:],
+                in_=v[0, first : first + UNIT_HEADS, w].rearrange("h (p j) d -> p h (j d)", j=PACK),
+            )
 
-        def load_a(u, lo, hi):
-            w, h0 = u // UPW, UH * (u % UPW)
-            nc.sync.dma_start(out=ab[u][:, lo:hi, :], in_=attn_bytes[0, h0 + lo : h0 + hi, w].rearrange("h q k -> q h k"))
+        w_words = keep.tile([P, 2, 2 * CHANNELS], U8, align_bytes=64)
+        bias = keep.tile([P, CHANNELS], BF16, align_bytes=64)
 
-        wt = keep.tile([P, 2, 2 * D], U8, align_bytes=64)
-        bias = keep.tile([P, D], BF16, align_bytes=64)
-        load_a(0, 0, 1)
-        load_a(0, 1, 2)
-        load_a(0, 2, 4)
-        load_a(1, 0, UH)
+        for h0, n in pieces(0):
+            load_attn(0, h0, n)
+        load_attn(1, 0, UNIT_HEADS)
         load_v(0)
         load_v(1)
-        for u in range(2, NU):
-            load_a(u, 0, UH)
+        for u in range(2, UNITS):
+            load_attn(u, 0, UNIT_HEADS)
             load_v(u)
-            if u == 7:
+            if u == WEIGHTS_BEHIND_UNIT:
                 for g in range(2):
-                    nc.sync.dma_start(out=wt[:, g, :].bitcast(I32), in_=w_words[g].bitcast(I32))
+                    nc.sync.dma_start(out=w_words[:, g, :].bitcast(I32), in_=proj_w_words[g].bitcast(I32))
                 for q in range(4):
                     nc.sync.dma_start(
-                        out=wsc[32 * q : 32 * q + 4, :, :].bitcast(I32),
-                        in_=w_scales[:, 4 * q : 4 * q + 4, :].rearrange("g r n -> r g n").bitcast(I32),
+                        out=w_scales[32 * q : 32 * q + 4, :, :].bitcast(I32),
+                        in_=proj_w_scales[:, 4 * q : 4 * q + 4, :].rearrange("g r n -> r g n").bitcast(I32),
                     )
-
         nc.sync.dma_start(out=bias[:], in_=proj_b.partition_broadcast(P))
 
         wide = {}
-        tp = {}
-        grp = {}
-        acodes = {}
-        vgrp = {}
-        vcodes = {}
-        o_ps = {}
-        obf = {}
-        ot = {}
-        ogrp = {}
-        mcodes = {}
-        fin = {}
-        res = {}
+        turned = {}
+        attn_grouped = {}
+        attn_codes = {}
+        v_grouped = {}
+        v_codes = {}
+        o_bank = {}
+        o_rows = {}
+        o_turned = {}
+        m_grouped = {}
+        m_codes = {}
+        projected = {}
 
-        def widen(u, h0, n, on_vector=False):
+        def widen(u, h0, n, engine_copy):
             if h0 == 0:
-                wide[u] = rot.tile([P, UH, SEQ], BF16, name="wide", align_bytes=64, bufs=4)
-            dst = wide[u][:, h0 : h0 + n, :].rearrange("p h k -> p (h k)")
-            src = ab[u][:, h0 : h0 + n, :].rearrange("p h k -> p (h k)").bitcast(FP8)
-            if on_vector:
-                nc.vector.tensor_copy(out=dst, in_=src)
-            else:
-                nc.scalar.copy(out=dst, in_=src)
+                wide[u] = work.tile([P, UNIT_HEADS, KEYS], BF16, name="wide", align_bytes=64, bufs=4)
+            engine_copy(
+                out=wide[u][:, h0 : h0 + n, :].rearrange("p h k -> p (h k)"),
+                in_=codes_in[u][:, h0 : h0 + n, :].rearrange("p h k -> p (h k)").bitcast(FP8),
+            )
 
         def turn(u, h0, n):
             words = wide[u][:].rearrange("p h k -> p (h k)").bitcast(F32)
-            t = psum.tile([P, 2, 2, P], F32, name="tp", bufs=4)
-            tp[u, h0] = t
+            bank = psum.tile([P, 2, 2, P], F32, name="bank", bufs=4)
+            turned[u, h0] = bank
             for i in range(n):
-                h = h0 + i
+                first, end = KEYS // 2 * (h0 + i), KEYS // 2 * (h0 + i + 1)
                 for e in range(2):
-                    nc.tensor.transpose(t[:, e, i, :], words[:, 256 * h + e : 256 * (h + 1) : 2], ident[:])
+                    nc.tensor.transpose(bank[:, e, i, :], words[:, first + e : end : 2], identity[:])
 
-        def group_tile(u):
-            if u not in grp:
-                grp[u] = rot.tile([P, UH * P, 2, 2], BF16, name="grp", align_bytes=64)
+        def grouped_columns(u, h0, n):
+            if u not in attn_grouped:
+                attn_grouped[u] = work.tile([P, UNIT_HEADS * QUERIES, 2, 2], BF16, name="attn_grouped", align_bytes=64)
+            return attn_grouped[u][:, QUERIES * h0 : QUERIES * (h0 + n)]
+
+        def bank_keys(u, h0):
+            bank = turned[u, h0][:].rearrange("p u h r -> p u (h r)").bitcast(BF16)
+            return bank.rearrange("p u (r e) -> p u r e", e=2)
 
         def product(u, h0, n):
-            group_tile(u)
-            src = tp[u, h0][:].rearrange("p u h r -> p u (h r)").bitcast(BF16).rearrange("p u (r e) -> p r u e", e=2)
+            columns = QUERIES * n
             nc.vector.tensor_tensor(
-                out=grp[u][:, P * h0 : P * (h0 + n)],
-                in0=src[:, : P * n],
-                in1=scale[:].to_broadcast([P, P * n, 2, 2]),
+                out=grouped_columns(u, h0, n),
+                in0=bank_keys(u, h0).rearrange("p u r e -> p r u e")[:, :columns],
+                in1=key_scale[:].to_broadcast([P, columns, 2, 2]),
                 op=MULT,
             )
 
-        def product_planes(u, h0, n, engine):
-            group_tile(u)
-            t = rot.tile([P, 4, P * n], BF16, name="planes", align_bytes=64)
-            src = tp[u, h0][:].rearrange("p u h r -> p u (h r)").bitcast(BF16).rearrange("p u (r e) -> p u e r", e=2)
-            for j in range(4):
+        def product_on_scalar(u, h0, n):
+            columns = QUERIES * n
+            by_t = work.tile([P, PACK, columns], BF16, name="by_t", align_bytes=64)
+            keys = bank_keys(u, h0)
+            for t in range(PACK):
+                half, e = t // 2, t % 2
                 nc.scalar.activation(
-                    out=t[:, j, :],
-                    in_=src[:, j // 2, j % 2, : P * n],
+                    out=by_t[:, t, :],
+                    in_=keys[:, half, :columns, e],
                     func=COPY,
-                    scale=scale[:, 0, j // 2, j % 2 : j % 2 + 1],
+                    scale=key_scale[:, 0, half, e : e + 1],
                 )
-            dst = grp[u][:, P * h0 : P * (h0 + n)].rearrange("p r u e -> p r (u e)")
-            pl = t[:].rearrange("p j r -> p r j")
-            if engine == "scalar":
-                nc.scalar.copy(out=dst, in_=pl)
-            elif engine == "vector":
-                nc.vector.tensor_copy(out=dst, in_=pl)
-            else:
-                nc.gpsimd.tensor_scalar(out=dst, in0=pl, scalar1=1.0, scalar2=0.0, op0=MULT, op1=ADD)
-
-        def quant_attn(u, h0, n):
-            if h0 == 0:
-                c = rot.tile([P, UH * P], U32, name="ac", align_bytes=64)
-                s = rot.tile([P, UH * P], U8, name="asc", align_bytes=64)
-                acodes[u] = (c, s)
-            c, s = acodes[u]
-            cols = slice(P * h0, P * (h0 + n))
-            nc.vector.quantize_mx(
-                out=c[:, cols].bitcast(FP8X4),
-                scales=s[:, cols],
-                in_=grp[u][:, P * h0 : P * (h0 + n)].rearrange("p r u e -> p (r u e)"),
+            nc.scalar.copy(
+                out=grouped_columns(u, h0, n).rearrange("p r u e -> p r (u e)"), in_=by_t[:].rearrange("p t r -> p r t")
             )
 
-        def inter_v(u, engine):
-            t = rot.tile([P, UH, HD, 4], BF16, name="vgrp" if engine == "gpsimd" else "vgrp_last", align_bytes=64, bufs=2)
-            vgrp[u] = t
-            src = vraw[u][:].rearrange("p h (j d) -> p h d j", j=4)
-            if engine == "vector":
-                nc.vector.tensor_copy(out=t[:], in_=src)
-            elif engine == "scalar":
-                nc.scalar.copy(out=t[:], in_=src)
-            else:
-                nc.gpsimd.tensor_scalar(out=t[:], in0=src, scalar1=1.0, scalar2=0.0, op0=MULT, op1=ADD)
-
-        def quant_v(u):
-            c = rot.tile([P, UH * HD], U32, name="vc", align_bytes=64, bufs=4)
-            s = rot.tile([P, UH * HD], U8, name="vsc", align_bytes=64, bufs=4)
-            vcodes[u] = (c, s)
+        def quantise_attn(u, h0, n):
+            if h0 == 0:
+                words = work.tile([P, UNIT_HEADS * QUERIES], U32, name="attn_words", align_bytes=64)
+                scales = work.tile([P, UNIT_HEADS * QUERIES], U8, name="attn_scales", align_bytes=64)
+                attn_codes[u] = (words, scales)
+            words, scales = attn_codes[u]
+            columns = slice(QUERIES * h0, QUERIES * (h0 + n))
             nc.vector.quantize_mx(
-                out=c[:].bitcast(FP8X4), scales=s[:], in_=vgrp[u][:].rearrange("p h d j -> p (h d j)")
+                out=words[:, columns].bitcast(FP8X4),
+                scales=scales[:, columns],
+                in_=attn_grouped[u][:, columns].rearrange("p r u e -> p (r u e)"),
+            )
+
+        def interleave_v(u):
+            rows = v_rows[u][:].rearrange("p h (j d) -> p h d j", j=PACK)
+            if u < LAST:
+                grouped = work.tile([P, UNIT_HEADS, HEAD_DIM, PACK], BF16, name="v_grouped", align_bytes=64, bufs=2)
+                nc.gpsimd.tensor_scalar(out=grouped[:], in0=rows, scalar1=1.0, scalar2=0.0, op0=MULT, op1=ADD)
+            else:
+                grouped = keep.tile([P, UNIT_HEADS, HEAD_DIM, PACK], BF16, name="v_grouped_last", align_bytes=64)
+                nc.scalar.copy(out=grouped[:], in_=rows)
+            v_grouped[u] = grouped
+
+        def quantise_v(u):
+            words = work.tile([P, UNIT_HEADS * HEAD_DIM], U32, name="v_words", align_bytes=64, bufs=4)
+            scales = work.tile([P, UNIT_HEADS * HEAD_DIM], U8, name="v_scales", align_bytes=64, bufs=4)
+            v_codes[u] = (words, scales)
+            nc.vector.quantize_mx(
+                out=words[:].bitcast(FP8X4), scales=scales[:], in_=v_grouped[u][:].rearrange("p h d j -> p (h d j)")
             )
 
         def mix(u, h0, n):
             g = u // 2
             if u % 2 == 0 and h0 == 0:
-                o_ps[g] = psum.tile([P, 8 * HD], F32, name="o_ps", bufs=1)
-            ac, asc = acodes[u]
-            vc, vsc = vcodes[u]
+                o_bank[g] = psum.tile([P, GROUP_HEADS * HEAD_DIM], F32, name="o_bank", bufs=1)
+            a_words, a_scales = attn_codes[u]
+            v_words, v_scales = v_codes[u]
             for h in range(h0, h0 + n):
-                hh = UH * (u % 2) + h
-                q = slice(P * h, P * (h + 1))
-                d = slice(HD * h, HD * (h + 1))
+                place = HEAD_DIM * (UNIT_HEADS * (u % 2) + h)
+                a = slice(QUERIES * h, QUERIES * (h + 1))
+                d = slice(HEAD_DIM * h, HEAD_DIM * (h + 1))
                 nc.tensor.matmul_mx(
-                    out=o_ps[g][:, HD * hh : HD * (hh + 1)],
-                    lhsT=ac[:, q].bitcast(FP8X4),
-                    lhsT_scale=asc[:, q],
-                    rhs=vc[:, d].bitcast(FP8X4),
-                    rhs_scale=vsc[:, d],
+                    out=o_bank[g][:, place : place + HEAD_DIM],
+                    lhsT=a_words[:, a].bitcast(FP8X4),
+                    lhsT_scale=a_scales[:, a],
+                    rhs=v_words[:, d].bitcast(FP8X4),
+                    rhs_scale=v_scales[:, d],
                     start=True,
                     stop=True,
                 )
 
         def empty_o(g, h0, n):
             if h0 == 0:
-                obf[g] = rot.tile([P, 8 * HD], BF16, name="obf", align_bytes=64, bufs=2)
-            cols = slice(HD * h0, HD * (h0 + n))
-            nc.scalar.copy(out=obf[g][:, cols], in_=o_ps[g][:, cols])
+                o_rows[g] = work.tile([P, GROUP_HEADS * HEAD_DIM], BF16, name="o_rows", align_bytes=64, bufs=2)
+            columns = slice(HEAD_DIM * h0, HEAD_DIM * (h0 + n))
+            nc.scalar.copy(out=o_rows[g][:, columns], in_=o_bank[g][:, columns])
 
         def turn_o(g):
-            t = psum.tile([P, 2, P], F32, name="ot", bufs=1)
-            ot[g] = t
-            words = obf[g][:].bitcast(F32)
+            bank = psum.tile([P, 2, P], F32, name="o_turned", bufs=1)
+            o_turned[g] = bank
+            words = o_rows[g][:].bitcast(F32)
             for e in range(2):
-                nc.tensor.transpose(t[:, e, :], words[:, e::2], ident[:])
+                nc.tensor.transpose(bank[:, e, :], words[:, e::2], identity[:])
 
-        def empty_ot(g):
-            t = rot.tile([P, P, 2], F32, name="ogrp", align_bytes=64, bufs=2)
-            ogrp[g] = t
-            nc.scalar.copy(out=t[:], in_=ot[g][:].rearrange("p e r -> p r e"))
+        def empty_turned_o(g):
+            m_grouped[g] = work.tile([P, QUERIES, 2], F32, name="m_grouped", align_bytes=64, bufs=2)
+            nc.scalar.copy(out=m_grouped[g][:], in_=o_turned[g][:].rearrange("p e r -> p r e"))
 
-        def quant_o(g):
-            c = rot.tile([P, P], U32, name="mc", align_bytes=64)
-            s = rot.tile([P, P], U8, name="msc", align_bytes=64)
-            mcodes[g] = (c, s)
+        def quantise_m(g):
+            words = work.tile([P, QUERIES], U32, name="m_words", align_bytes=64)
+            scales = work.tile([P, QUERIES], U8, name="m_scales", align_bytes=64)
+            m_codes[g] = (words, scales)
             nc.vector.quantize_mx(
-                out=c[:].bitcast(FP8X4), scales=s[:], in_=ogrp[g][:].rearrange("p r e -> p (r e)").bitcast(BF16)
+                out=words[:].bitcast(FP8X4),
+                scales=scales[:],
+                in_=m_grouped[g][:].rearrange("p r e -> p (r e)").bitcast(BF16),
             )
 
         def project(g):
-            w, gg = g // 2, g % 2
-            c, s = mcodes[g]
+            w, k_pass = g // 2, g % 2
+            words, scales = m_codes[g]
             for n in range(2):
-                if gg == 0:
-                    if w < 2:
-                        fin[w, n] = psum.tile([P, 512], F32, name=f"fin{n}", bufs=1)
+                if k_pass == 0:
+                    if w < WINDOWS - 1:
+                        projected[w, n] = psum.tile([P, BANK], F32, name=f"projected{n}", bufs=1)
                     else:
-                        fin[w, n] = psum.tile([P, 512], F32, name="tp", bufs=4)
+                        projected[w, n] = psum.tile([P, BANK], F32, name="bank", bufs=4)
                 nc.tensor.matmul_mx(
-                    out=fin[w, n][:],
-                    lhsT=c[:].bitcast(FP8X4),
-                    lhsT_scale=s[:],
-                    rhs=wt[:, gg, 1024 * n : 1024 * (n + 1)].bitcast(FP4X4),
-                    rhs_scale=wsc[:, gg, 512 * n : 512 * (n + 1)],
-                    start=(gg == 0),
-                    stop=(gg == 1),
+                    out=projected[w, n][:],
+                    lhsT=words[:].bitcast(FP8X4),
+                    lhsT_scale=scales[:],
+                    rhs=w_words[:, k_pass, 2 * BANK * n : 2 * BANK * (n + 1)].bitcast(FP4X4),
+                    rhs_scale=w_scales[:, k_pass, BANK * n : BANK * (n + 1)],
+                    start=(k_pass == 0),
+                    stop=(k_pass == 1),
                 )
 
-        out_w = out[0].rearrange("(i w) n -> w i n", w=NWIN)
+        def stage(w, n):
+            staged = keep.tile([P, BANK], F32, name=f"staged{w}{n}", align_bytes=64)
+            nc.scalar.copy(out=staged[:], in_=projected[w, n][:])
+            projected[w, n] = staged
 
-        def copy_fin(w, n):
-            t = rot.tile([P, 512], F32, name=f"raw{w}{n}", align_bytes=64, bufs=1)
-            fin[w, n, "sb"] = t
-            nc.scalar.copy(out=t[:], in_=fin[w, n][:])
+        out_rows = out[0].rearrange("(i w) n -> w i n", w=WINDOWS)
 
-        def finish(w, n):
-            cols = slice(512 * n, 512 * (n + 1))
-            t = rot.tile([P, 512], F32, name=f"res{w}{n}", align_bytes=64, bufs=1)
-            src = fin[w, n, "sb"] if w == 0 else fin[w, n]
-            nc.vector.tensor_tensor(out=t[:], in0=src[:], in1=bias[:, cols], op=ADD)
-            nc.sync.dma_start(out=out_w[w, :, cols], in_=t[:])
+        def finish(w, c0, c1):
+            n = c0 // BANK
+            result = keep.tile([P, c1 - c0], F32, name=f"result{w}_{c0}", align_bytes=64)
+            nc.vector.tensor_tensor(
+                out=result[:], in0=projected[w, n][:, c0 - BANK * n : c1 - BANK * n], in1=bias[:, c0:c1], op=ADD
+            )
+            nc.sync.dma_start(out=out_rows[w, :, c0:c1], in_=result[:])
 
-        def pieces(u):
-            if u in SPLIT:
-                return SPLIT[u]
-            if u == 0:
-                return [(0, 1, "v"), (1, 1, "v"), (2, 2, "v")]
-            if u == NU - 1:
-                return [(0, 2, "v"), (2, 1, "v"), (3, 1, "v")]
-            return [(0, 2, "v"), (2, 2, "v")]
-
-        widen(0, 0, 1, True)
-        widen(0, 1, 1)
+        vector_copy, scalar_copy = nc.vector.tensor_copy, nc.scalar.copy
+        widen(0, 0, 1, vector_copy)
+        widen(0, 1, 1, scalar_copy)
         turn(0, 0, 1)
         turn(0, 1, 1)
-        widen(0, 2, 1, True)
-        widen(0, 3, 1)
+        widen(0, 2, 1, vector_copy)
+        widen(0, 3, 1, scalar_copy)
         turn(0, 2, 2)
-        inter_v(0, "gpsimd")
-        inter_v(1, "gpsimd")
-        widen(1, 0, 2)
-        widen(1, 2, 2)
-        for s in range(NU):
-            odd = s % 2 == 1
-            g = (s - 3) // 2 if odd and s >= 3 else None
-            gq = (s - 4) // 2 if not odd and s >= 4 else None
-            gp = {6: 0, 7: 1, 9: 2, 11: 3}.get(s)
-            if s + 1 < NU:
-                for h0, n, e in pieces(s + 1):
+        interleave_v(0)
+        interleave_v(1)
+        widen(1, 0, 2, scalar_copy)
+        widen(1, 2, 2, scalar_copy)
+        for s in range(UNITS):
+            o_group = (s - 3) // 2 if s % 2 == 1 and s >= 3 else None
+            m_group = (s - 4) // 2 if s % 2 == 0 and s >= 4 else None
+            if s + 1 < UNITS:
+                for h0, n in pieces(s + 1):
                     turn(s + 1, h0, n)
-            if s + 2 < NU:
-                widen(s + 2, 0, 2)
-            if gp is not None:
-                project(gp)
-            if g is not None:
-                empty_o(g, 0, 8)
-                turn_o(g)
-            if s + 2 < NU:
-                widen(s + 2, 2, 2)
-            for h0, n, e in pieces(s):
-                if e != "v":
-                    product_planes(s, h0, n, e)
-            if g is not None:
-                empty_ot(g)
-            if gp == 1:
-                copy_fin(0, 0)
-                copy_fin(0, 1)
-            if s == NU - 2:
-                inter_v(NU - 1, "scalar")
-            for h0, n, e in pieces(s):
-                if e == "v" and (s < NU - 1 or h0 == 0):
+            if s + 2 < UNITS:
+                widen(s + 2, 0, 2, scalar_copy)
+            if s in PROJECT_IN_STEP:
+                project(PROJECT_IN_STEP[s])
+            if o_group is not None:
+                empty_o(o_group, 0, GROUP_HEADS)
+                turn_o(o_group)
+            if s + 2 < UNITS:
+                widen(s + 2, 2, 2, scalar_copy)
+            if o_group is not None:
+                empty_turned_o(o_group)
+            for h0, n in pieces(s):
+                if on_scalar(s, h0):
+                    product_on_scalar(s, h0, n)
+            if s == 7:
+                stage(0, 0)
+            if s == 8:
+                stage(0, 1)
+            if s + 1 == LAST:
+                interleave_v(LAST)
+            for h0, n in pieces(s):
+                if not on_scalar(s, h0) and (s < LAST or h0 == 0):
                     product(s, h0, n)
-            if gq is not None:
-                quant_o(gq)
             if s > 0:
-                quant_attn(s - 1, 0, UH)
-                quant_v(s - 1)
-                mix(s - 1, 0, UH)
-            if s + 2 < NU - 1:
-                inter_v(s + 2, "gpsimd")
+                quantise_attn(s - 1, 0, UNIT_HEADS)
+            if m_group is not None:
+                quantise_m(m_group)
+            if s > 0:
+                quantise_v(s - 1)
+                mix(s - 1, 0, UNIT_HEADS)
+            if s + 2 < LAST:
+                interleave_v(s + 2)
 
-        u, g = NU - 1, NU // 2 - 1
-        if pieces(u)[1][2] == "v":
-            product(u, 2, 1)
-        quant_o(g - 1)
-        quant_v(u)
-        quant_attn(u, 0, 2)
+        g = GROUPS - 1
+        product(LAST, 2, 1)
+        quantise_v(LAST)
+        quantise_m(g - 1)
+        quantise_attn(LAST, 0, 2)
         project(g - 1)
-        mix(u, 0, 2)
-        product(u, 3, 1)
-        quant_attn(u, 2, 1)
-        mix(u, 2, 1)
-        quant_attn(u, 3, 1)
-        mix(u, 3, 1)
+        mix(LAST, 0, 2)
+        product(LAST, 3, 1)
+        quantise_attn(LAST, 2, 1)
+        mix(LAST, 2, 1)
+        quantise_attn(LAST, 3, 1)
+        mix(LAST, 3, 1)
         empty_o(g, 0, 4)
         empty_o(g, 4, 2)
         empty_o(g, 6, 2)
-        finish(0, 0)
-        finish(0, 1)
+        finish(0, 0, BANK)
+        finish(0, BANK, CHANNELS)
         turn_o(g)
-        empty_ot(g)
-        finish(1, 0)
-        quant_o(g)
+        empty_turned_o(g)
+        finish(1, 0, BANK)
+        quantise_m(g)
         project(g)
-        finish(1, 1)
-        finish(2, 0)
-        finish(2, 1)
+        finish(1, BANK, CHANNELS)
+        finish(2, 0, BANK)
+        finish(2, BANK, BANK + BANK // 2)
+        finish(2, BANK + BANK // 2, CHANNELS)

from contextlib import ExitStack

import concourse.mybir as mybir
from concourse.masks import make_identity

HEADS, WINDOWS, QUERIES, KEYS, HEAD_DIM, CHANNELS = 16, 3, 128, 512, 64, 1024

FLOPS = 2 * HEADS * WINDOWS * QUERIES * KEYS * HEAD_DIM + 2 * WINDOWS * QUERIES * CHANNELS * CHANNELS

F32 = mybir.dt.float32
BF16 = mybir.dt.bfloat16
I32 = mybir.dt.int32
U32 = mybir.dt.uint32
U8 = mybir.dt.uint8
FP8 = mybir.dt.float8_e4m3fn
FP8X4 = mybir.dt.float8_e4m3fn_x4
FP4X4 = mybir.dt.float4_e2m1fn_x4
MULT = mybir.AluOpType.mult
ADD = mybir.AluOpType.add
COPY = mybir.ActivationFunctionType.Copy

P = 128
PACK = 4
BANK = 512

UNIT_HEADS = 4
GROUP_HEADS = 8
UNITS = WINDOWS * HEADS // UNIT_HEADS
GROUPS = UNITS // 2
LAST = UNITS - 1

PIECES = {0: ((0, 1), (1, 1), (2, 2)), LAST: ((0, 2), (2, 1), (3, 1))}
USUAL_PIECES = ((0, 2), (2, 2))
SHARED_UNITS = (5, 10)
SHARED_PIECES = ((0, 2), (2, 1), (3, 1))
WEIGHTS_BEHIND_UNIT = 7
PROJECT_IN_STEP = {6: 0, 7: 1, 9: 2, 11: 3}


def pieces(u):
    if u in SHARED_UNITS:
        return SHARED_PIECES
    return PIECES.get(u, USUAL_PIECES)


def on_scalar(u, h0):
    return u in SHARED_UNITS and h0 == UNIT_HEADS - 1


def tile_hieramaskunitattention_pb_w4_kernel(
    tc, attn_bytes, attn_scale, v, proj_w_words, proj_w_scales, proj_b, out
):
    nc = tc.nc
    with ExitStack() as ctx:
        keep = ctx.enter_context(tc.tile_pool(name="keep", bufs=1))
        work = ctx.enter_context(tc.tile_pool(name="work", bufs=3))
        psum = ctx.enter_context(tc.psum_pool(name="psum", bufs=1))
        ctx.enter_context(tc.manual_schedule())

        identity = keep.tile([P, P], F32)
        make_identity(nc, identity[:])

        w_scales = keep.tile([P, 2, CHANNELS], U8, align_bytes=64)
        nc.vector.memset(w_scales[:].rearrange("p g n -> p (g n)").bitcast(I32), 0)

        key_scale = keep.tile([P, 1, 2, 2], F32, align_bytes=64)
        nc.scalar.dma_start(
            out=key_scale[:].rearrange("p o u e -> p (o u e)"),
            in_=attn_scale.rearrange("a b c d (p t) -> p (a b c d t)", t=PACK),
        )

        codes_in = []
        v_rows = []
        for u in range(UNITS):
            codes_in.append(keep.tile([P, UNIT_HEADS, KEYS], U8, name=f"codes_in{u}", align_bytes=64))
            v_rows.append(keep.tile([P, UNIT_HEADS, PACK * HEAD_DIM], BF16, name=f"v_rows{u}", align_bytes=64))

        def load_attn(u, h0, n):
            w, first = u // 4, UNIT_HEADS * (u % 4) + h0
            nc.sync.dma_start(
                out=codes_in[u][:, h0 : h0 + n, :],
                in_=attn_bytes[0, first : first + n, w].rearrange("h q k -> q h k"),
            )

        def load_v(u):
            w, first = u // 4, UNIT_HEADS * (u % 4)
            nc.sync.dma_start(
                out=v_rows[u][:],
                in_=v[0, first : first + UNIT_HEADS, w].rearrange("h (p j) d -> p h (j d)", j=PACK),
            )

        w_words = keep.tile([P, 2, 2 * CHANNELS], U8, align_bytes=64)
        bias = keep.tile([P, CHANNELS], BF16, align_bytes=64)

        for h0, n in pieces(0):
            load_attn(0, h0, n)
        load_attn(1, 0, UNIT_HEADS)
        load_v(0)
        load_v(1)
        for u in range(2, UNITS):
            load_attn(u, 0, UNIT_HEADS)
            load_v(u)
            if u == WEIGHTS_BEHIND_UNIT:
                for g in range(2):
                    nc.sync.dma_start(out=w_words[:, g, :].bitcast(I32), in_=proj_w_words[g].bitcast(I32))
                for q in range(4):
                    nc.sync.dma_start(
                        out=w_scales[32 * q : 32 * q + 4, :, :].bitcast(I32),
                        in_=proj_w_scales[:, 4 * q : 4 * q + 4, :].rearrange("g r n -> r g n").bitcast(I32),
                    )
        nc.sync.dma_start(out=bias[:], in_=proj_b.partition_broadcast(P))

        wide = {}
        turned = {}
        attn_grouped = {}
        attn_codes = {}
        v_grouped = {}
        v_codes = {}
        o_bank = {}
        o_rows = {}
        o_turned = {}
        m_grouped = {}
        m_codes = {}
        projected = {}

        def widen(u, h0, n, engine_copy):
            if h0 == 0:
                wide[u] = work.tile([P, UNIT_HEADS, KEYS], BF16, name="wide", align_bytes=64, bufs=4)
            engine_copy(
                out=wide[u][:, h0 : h0 + n, :].rearrange("p h k -> p (h k)"),
                in_=codes_in[u][:, h0 : h0 + n, :].rearrange("p h k -> p (h k)").bitcast(FP8),
            )

        def turn(u, h0, n):
            words = wide[u][:].rearrange("p h k -> p (h k)").bitcast(F32)
            bank = psum.tile([P, 2, 2, P], F32, name="bank", bufs=4)
            turned[u, h0] = bank
            for i in range(n):
                first, end = KEYS // 2 * (h0 + i), KEYS // 2 * (h0 + i + 1)
                for e in range(2):
                    nc.tensor.transpose(bank[:, e, i, :], words[:, first + e : end : 2], identity[:])

        def grouped_columns(u, h0, n):
            if u not in attn_grouped:
                attn_grouped[u] = work.tile([P, UNIT_HEADS * QUERIES, 2, 2], BF16, name="attn_grouped", align_bytes=64)
            return attn_grouped[u][:, QUERIES * h0 : QUERIES * (h0 + n)]

        def bank_keys(u, h0):
            bank = turned[u, h0][:].rearrange("p u h r -> p u (h r)").bitcast(BF16)
            return bank.rearrange("p u (r e) -> p u r e", e=2)

        def product(u, h0, n):
            columns = QUERIES * n
            nc.vector.tensor_tensor(
                out=grouped_columns(u, h0, n),
                in0=bank_keys(u, h0).rearrange("p u r e -> p r u e")[:, :columns],
                in1=key_scale[:].to_broadcast([P, columns, 2, 2]),
                op=MULT,
            )

        def product_on_scalar(u, h0, n):
            columns = QUERIES * n
            by_t = work.tile([P, PACK, columns], BF16, name="by_t", align_bytes=64)
            keys = bank_keys(u, h0)
            for t in range(PACK):
                half, e = t // 2, t % 2
                nc.scalar.activation(
                    out=by_t[:, t, :],
                    in_=keys[:, half, :columns, e],
                    func=COPY,
                    scale=key_scale[:, 0, half, e : e + 1],
                )
            nc.scalar.copy(
                out=grouped_columns(u, h0, n).rearrange("p r u e -> p r (u e)"), in_=by_t[:].rearrange("p t r -> p r t")
            )

        def quantise_attn(u, h0, n):
            if h0 == 0:
                words = work.tile([P, UNIT_HEADS * QUERIES], U32, name="attn_words", align_bytes=64)
                scales = work.tile([P, UNIT_HEADS * QUERIES], U8, name="attn_scales", align_bytes=64)
                attn_codes[u] = (words, scales)
            words, scales = attn_codes[u]
            columns = slice(QUERIES * h0, QUERIES * (h0 + n))
            nc.vector.quantize_mx(
                out=words[:, columns].bitcast(FP8X4),
                scales=scales[:, columns],
                in_=attn_grouped[u][:, columns].rearrange("p r u e -> p (r u e)"),
            )

        def interleave_v(u):
            rows = v_rows[u][:].rearrange("p h (j d) -> p h d j", j=PACK)
            if u < LAST:
                grouped = work.tile([P, UNIT_HEADS, HEAD_DIM, PACK], BF16, name="v_grouped", align_bytes=64, bufs=2)
                nc.gpsimd.tensor_scalar(out=grouped[:], in0=rows, scalar1=1.0, scalar2=0.0, op0=MULT, op1=ADD)
            else:
                grouped = keep.tile([P, UNIT_HEADS, HEAD_DIM, PACK], BF16, name="v_grouped_last", align_bytes=64)
                nc.scalar.copy(out=grouped[:], in_=rows)
            v_grouped[u] = grouped

        def quantise_v(u):
            words = work.tile([P, UNIT_HEADS * HEAD_DIM], U32, name="v_words", align_bytes=64, bufs=4)
            scales = work.tile([P, UNIT_HEADS * HEAD_DIM], U8, name="v_scales", align_bytes=64, bufs=4)
            v_codes[u] = (words, scales)
            nc.vector.quantize_mx(
                out=words[:].bitcast(FP8X4), scales=scales[:], in_=v_grouped[u][:].rearrange("p h d j -> p (h d j)")
            )

        def mix(u, h0, n):
            g = u // 2
            if u % 2 == 0 and h0 == 0:
                o_bank[g] = psum.tile([P, GROUP_HEADS * HEAD_DIM], F32, name="o_bank", bufs=1)
            a_words, a_scales = attn_codes[u]
            v_words, v_scales = v_codes[u]
            for h in range(h0, h0 + n):
                place = HEAD_DIM * (UNIT_HEADS * (u % 2) + h)
                a = slice(QUERIES * h, QUERIES * (h + 1))
                d = slice(HEAD_DIM * h, HEAD_DIM * (h + 1))
                nc.tensor.matmul_mx(
                    out=o_bank[g][:, place : place + HEAD_DIM],
                    lhsT=a_words[:, a].bitcast(FP8X4),
                    lhsT_scale=a_scales[:, a],
                    rhs=v_words[:, d].bitcast(FP8X4),
                    rhs_scale=v_scales[:, d],
                    start=True,
                    stop=True,
                )

        def empty_o(g, h0, n):
            if h0 == 0:
                o_rows[g] = work.tile([P, GROUP_HEADS * HEAD_DIM], BF16, name="o_rows", align_bytes=64, bufs=2)
            columns = slice(HEAD_DIM * h0, HEAD_DIM * (h0 + n))
            nc.scalar.copy(out=o_rows[g][:, columns], in_=o_bank[g][:, columns])

        def turn_o(g):
            bank = psum.tile([P, 2, P], F32, name="o_turned", bufs=1)
            o_turned[g] = bank
            words = o_rows[g][:].bitcast(F32)
            for e in range(2):
                nc.tensor.transpose(bank[:, e, :], words[:, e::2], identity[:])

        def empty_turned_o(g):
            m_grouped[g] = work.tile([P, QUERIES, 2], F32, name="m_grouped", align_bytes=64, bufs=2)
            nc.scalar.copy(out=m_grouped[g][:], in_=o_turned[g][:].rearrange("p e r -> p r e"))

        def quantise_m(g):
            words = work.tile([P, QUERIES], U32, name="m_words", align_bytes=64)
            scales = work.tile([P, QUERIES], U8, name="m_scales", align_bytes=64)
            m_codes[g] = (words, scales)
            nc.vector.quantize_mx(
                out=words[:].bitcast(FP8X4),
                scales=scales[:],
                in_=m_grouped[g][:].rearrange("p r e -> p (r e)").bitcast(BF16),
            )

        def project(g):
            w, k_pass = g // 2, g % 2
            words, scales = m_codes[g]
            for n in range(2):
                if k_pass == 0:
                    if w < WINDOWS - 1:
                        projected[w, n] = psum.tile([P, BANK], F32, name=f"projected{n}", bufs=1)
                    else:
                        projected[w, n] = psum.tile([P, BANK], F32, name="bank", bufs=4)
                nc.tensor.matmul_mx(
                    out=projected[w, n][:],
                    lhsT=words[:].bitcast(FP8X4),
                    lhsT_scale=scales[:],
                    rhs=w_words[:, k_pass, 2 * BANK * n : 2 * BANK * (n + 1)].bitcast(FP4X4),
                    rhs_scale=w_scales[:, k_pass, BANK * n : BANK * (n + 1)],
                    start=(k_pass == 0),
                    stop=(k_pass == 1),
                )

        def stage(w, n):
            staged = keep.tile([P, BANK], F32, name=f"staged{w}{n}", align_bytes=64)
            nc.scalar.copy(out=staged[:], in_=projected[w, n][:])
            projected[w, n] = staged

        out_rows = out[0].rearrange("(i w) n -> w i n", w=WINDOWS)

        def finish(w, c0, c1):
            n = c0 // BANK
            result = keep.tile([P, c1 - c0], F32, name=f"result{w}_{c0}", align_bytes=64)
            nc.vector.tensor_tensor(
                out=result[:], in0=projected[w, n][:, c0 - BANK * n : c1 - BANK * n], in1=bias[:, c0:c1], op=ADD
            )
            nc.sync.dma_start(out=out_rows[w, :, c0:c1], in_=result[:])

        vector_copy, scalar_copy = nc.vector.tensor_copy, nc.scalar.copy
        widen(0, 0, 1, vector_copy)
        widen(0, 1, 1, scalar_copy)
        turn(0, 0, 1)
        turn(0, 1, 1)
        widen(0, 2, 1, vector_copy)
        widen(0, 3, 1, scalar_copy)
        turn(0, 2, 2)
        interleave_v(0)
        interleave_v(1)
        widen(1, 0, 2, scalar_copy)
        widen(1, 2, 2, scalar_copy)
        for s in range(UNITS):
            o_group = (s - 3) // 2 if s % 2 == 1 and s >= 3 else None
            m_group = (s - 4) // 2 if s % 2 == 0 and s >= 4 else None
            if s + 1 < UNITS:
                for h0, n in pieces(s + 1):
                    turn(s + 1, h0, n)
            if s + 2 < UNITS:
                widen(s + 2, 0, 2, scalar_copy)
            if s in PROJECT_IN_STEP:
                project(PROJECT_IN_STEP[s])
            if o_group is not None:
                empty_o(o_group, 0, GROUP_HEADS)
                turn_o(o_group)
            if s + 2 < UNITS:
                widen(s + 2, 2, 2, scalar_copy)
            if o_group is not None:
                empty_turned_o(o_group)
            for h0, n in pieces(s):
                if on_scalar(s, h0):
                    product_on_scalar(s, h0, n)
            if s == 7:
                stage(0, 0)
            if s == 8:
                stage(0, 1)
            if s + 1 == LAST:
                interleave_v(LAST)
            for h0, n in pieces(s):
                if not on_scalar(s, h0) and (s < LAST or h0 == 0):
                    product(s, h0, n)
            if s > 0:
                quantise_attn(s - 1, 0, UNIT_HEADS)
            if m_group is not None:
                quantise_m(m_group)
            if s > 0:
                quantise_v(s - 1)
                mix(s - 1, 0, UNIT_HEADS)
            if s + 2 < LAST:
                interleave_v(s + 2)

        g = GROUPS - 1
        product(LAST, 2, 1)
        quantise_v(LAST)
        quantise_m(g - 1)
        quantise_attn(LAST, 0, 2)
        project(g - 1)
        mix(LAST, 0, 2)
        product(LAST, 3, 1)
        quantise_attn(LAST, 2, 1)
        mix(LAST, 2, 1)
        quantise_attn(LAST, 3, 1)
        mix(LAST, 3, 1)
        empty_o(g, 0, 4)
        empty_o(g, 4, 2)
        empty_o(g, 6, 2)
        finish(0, 0, BANK)
        finish(0, BANK, CHANNELS)
        turn_o(g)
        empty_turned_o(g)
        finish(1, 0, BANK)
        quantise_m(g)
        project(g)
        finish(1, BANK, CHANNELS)
        finish(2, 0, BANK)
        finish(2, BANK, BANK + BANK // 2)
        finish(2, BANK + BANK // 2, CHANNELS)
